import numpy as np
import ml_dtypes

BF16 = ml_dtypes.bfloat16


def bf(x):
    return np.asarray(x, np.float32).astype(BF16)


def f32(x):
    return np.asarray(x, np.float32)


def f64(x):
    return np.asarray(x).astype(np.float64)


def striped(idx):
    return np.tile(idx.reshape(-1, 16).T, (8, 1))


S, D, DM, M, N = 2048, 128, 256, 512, 512
EPS = 1e-6
TERMS = 150


def erf(a):
    c = np.clip(a, -6.0, 6.0)
    term = c.copy()
    total = c.copy()
    for i in range(1, TERMS):
        term = term * 2.0 * c * c / (2.0 * i + 1.0)
        total = total + term
    val = 2.0 / np.sqrt(np.pi) * np.exp(-c * c) * total
    return np.where(np.abs(a) <= 6.0, val, np.sign(a))


def setup_inputs():
    return {"x": bf(np.random.standard_normal((S, D))), "gain": f32(1.0 + 0.1 * np.random.standard_normal((D, 1))), "wup": bf(np.random.standard_normal((D, M)) / np.sqrt(D)), "bup": f32(0.1 * np.random.standard_normal((M, 1))), "wdown": bf(np.random.standard_normal((M, D)) / np.sqrt(M)), "bdown": f32(0.1 * np.random.standard_normal((D, 1))), "offs": striped(np.random.permutation(S)[:N])}


def reference(x, gain, wup, bup, wdown, bdown, offs):
    idx = offs[:16].T.reshape(-1)
    xs = f64(x)
    h = xs * f64(gain)[:, 0] / np.sqrt(np.sum(xs * xs, axis=1, keepdims=True) / DM + EPS)
    v = f64(wup).T @ h[idx].T + f64(bup)
    u = 0.5 * v * (1.0 + erf(v / np.sqrt(2.0)))
    return f64(wdown).T @ u + f64(bdown)

@@ -1,0 +1,114 @@
+import concourse.mybir as mybir
+from concourse.masks import make_identity
+
+S, D, M, N = 2048, 128, 512, 512
+P = 128
+STREAM_WIDTH = 256
+EPS = 1e-6
+FLOPS = 2 * D * M * N + 2 * M * D * N
+
+BF16, F32, U16 = mybir.dt.bfloat16, mybir.dt.float32, mybir.dt.uint16
+FUNC = mybir.ActivationFunctionType
+ALU = mybir.AluOpType
+
+BLOCKS = S // P
+CHUNK = 4
+CHUNKS = BLOCKS // CHUNK
+M_BLOCKS = M // P
+
+ROW_GAIN, ROW_BUP, ROW_BDOWN = 0, 1, 1 + M_BLOCKS
+
+
+def tile_transformerblock_kernel(tc, x, gain, wup, bup, wdown, bdown, offs, out):
+    nc = tc.nc
+    with (
+        tc.tile_pool(name="held", bufs=1) as held,
+        tc.tile_pool(name="squares", bufs=2) as squares,
+        tc.psum_pool(name="flipped", bufs=2) as flipped,
+        tc.psum_pool(name="hidden", bufs=4) as hidden,
+        tc.psum_pool(name="single", bufs=1) as single,
+    ):
+        offsets = held.tile([P, N // 16], U16, name="offsets")
+        nc.sync.dma_start(offsets[:], offs)
+
+        x_blocks = x.rearrange("(b p) d -> p b d", p=P)
+        x_chunks = []
+        for c in range(CHUNKS):
+            x_chunk = held.tile([P, CHUNK, D], BF16, name=f"x_chunk{c}")
+            queue = nc.sync if c % 2 == 0 else nc.scalar
+            queue.dma_start(x_chunk[:], x_blocks[:, c * CHUNK : (c + 1) * CHUNK, :])
+            x_chunks.append(x_chunk)
+
+        rows = held.tile([P, P], F32, name="rows")
+        nc.vector.memset(rows[:], 0.0)
+        nc.gpsimd.dma_start(rows[ROW_GAIN : ROW_GAIN + 1, :], gain.rearrange("d o -> o d"))
+        nc.gpsimd.dma_start(rows[ROW_BUP : ROW_BUP + M_BLOCKS, :], bup.rearrange("(r p) o -> r (p o)", p=P))
+        nc.gpsimd.dma_start(rows[ROW_BDOWN : ROW_BDOWN + 1, :], bdown.rearrange("d o -> o d"))
+
+        wup_sb = held.tile([D, M], BF16, name="wup_sb")
+        nc.gpsimd.dma_start(wup_sb[:], wup)
+        wdown_sb = held.tile([P, M_BLOCKS, D], BF16, name="wdown_sb")
+        nc.gpsimd.dma_start(wdown_sb[:], wdown.rearrange("(r p) c -> p r c", p=P))
+
+        identity = held.tile([P, P], F32, name="identity")
+        make_identity(nc, identity[:])
+        eps = held.tile([P, 1], F32, name="eps")
+        nc.vector.memset(eps[:], EPS)
+
+        columns_ps = single.tile([P, P], F32, name="columns_ps")
+        nc.tensor.transpose(columns_ps[:], rows[:], identity[:])
+        columns = held.tile([P, ROW_BDOWN + 1], F32, name="columns")
+        nc.vector.tensor_copy(columns[:], columns_ps[:, 0 : ROW_BDOWN + 1])
+        gain_col = columns[:, ROW_GAIN : ROW_GAIN + 1]
+        bdown_col = columns[:, ROW_BDOWN : ROW_BDOWN + 1]
+
+        sumsq = held.tile([P, 2, BLOCKS // 2], F32, name="sumsq")
+        for b in range(BLOCKS):
+            x_block = x_chunks[b // CHUNK][:, b % CHUNK, :]
+            total = sumsq[:, b % 2, b // 2 : b // 2 + 1]
+            if b % 2 == 0:
+                sq_scalar = squares.tile([P, D], F32, name="sq_scalar")
+                nc.scalar.activation(sq_scalar[:], x_block, FUNC.Square, accum_out=total)
+            else:
+                sq_vector = squares.tile([P, D], F32, name="sq_vector")
+                nc.vector.scalar_tensor_tensor(
+                    sq_vector[:], x_block, 1.0, x_block, ALU.mult, ALU.mult, accum_out=total
+                )
+
+        rms = held.tile([P, 2, BLOCKS // 2], F32, name="rms")
+        nc.scalar.activation(rms[:], sumsq[:], FUNC.Sqrt, bias=eps[:], scale=1.0 / STREAM_WIDTH)
+        rstd = held.tile([P, 2, BLOCKS // 2], F32, name="rstd")
+        nc.vector.reciprocal(rstd[:], rms[:])
+
+        table = held.tile([D, S], BF16, name="table")
+        for c in range(CHUNKS):
+            scaled = held.tile([P, CHUNK, D], F32, name=f"scaled{c}")
+            flipped_ps = flipped.tile([D, CHUNK * P], F32, name="flipped_ps")
+            for k in range(CHUNK):
+                b = c * CHUNK + k
+                rstd_col = rstd[:, b % 2, b // 2 : b // 2 + 1]
+                if b % 2 == 0:
+                    nc.scalar.activation(scaled[:, k, :], x_chunks[c][:, k, :], FUNC.Copy, scale=rstd_col)
+                else:
+                    nc.vector.tensor_scalar(scaled[:, k, :], x_chunks[c][:, k, :], rstd_col, None, ALU.mult)
+                nc.tensor.transpose(flipped_ps[:, k * P : (k + 1) * P], scaled[:, k, :], identity[:])
+            table_part = table[:, c * CHUNK * P : (c + 1) * CHUNK * P]
+            if c % 2 == 0:
+                nc.vector.tensor_scalar(table_part, flipped_ps[:], gain_col, None, ALU.mult)
+            else:
+                nc.scalar.activation(table_part, flipped_ps[:], FUNC.Copy, scale=gain_col)
+
+        out_ps = single.tile([D, N], F32, name="out_ps")
+        u = held.tile([P, M_BLOCKS, N], BF16, name="u")
+        for r in range(M_BLOCKS):
+            v_ps = hidden.tile([P, N], F32, name="v_ps")
+            nc.tensor.matmul(
+                v_ps[:], wup_sb[:, r * P : (r + 1) * P], table[:].indirect(offsets[:]), start=True, stop=True
+            )
+            bup_col = columns[:, ROW_BUP + r : ROW_BUP + r + 1]
+            nc.scalar.activation(u[:, r, :], v_ps[:], FUNC.Gelu, bias=bup_col)
+            nc.tensor.matmul(out_ps[:], wdown_sb[:, r, :], u[:, r, :], start=(r == 0), stop=(r == M_BLOCKS - 1))
+
+        result = held.tile([D, N], F32, name="result")
+        nc.vector.tensor_scalar(result[:], out_ps[:], bdown_col, None, ALU.add)
+        nc.sync.dma_start(out, result[:])

@@ -41,14 +41,14 @@ def tile_transformerblock_kernel(tc, x, gain, wup, bup, wdown, bdown, offs, out)
 
         rows = held.tile([P, P], F32, name="rows")
         nc.vector.memset(rows[:], 0.0)
-        nc.gpsimd.dma_start(rows[ROW_GAIN : ROW_GAIN + 1, :], gain.rearrange("d o -> o d"))
-        nc.gpsimd.dma_start(rows[ROW_BUP : ROW_BUP + M_BLOCKS, :], bup.rearrange("(r p) o -> r (p o)", p=P))
-        nc.gpsimd.dma_start(rows[ROW_BDOWN : ROW_BDOWN + 1, :], bdown.rearrange("d o -> o d"))
+        nc.sync.dma_start(rows[ROW_GAIN : ROW_GAIN + 1, :], gain.rearrange("d o -> o d"))
+        nc.sync.dma_start(rows[ROW_BUP : ROW_BUP + M_BLOCKS, :], bup.rearrange("(r p) o -> r (p o)", p=P))
+        nc.sync.dma_start(rows[ROW_BDOWN : ROW_BDOWN + 1, :], bdown.rearrange("d o -> o d"))
 
         wup_sb = held.tile([D, M], BF16, name="wup_sb")
-        nc.gpsimd.dma_start(wup_sb[:], wup)
+        nc.scalar.dma_start(wup_sb[:], wup)
         wdown_sb = held.tile([P, M_BLOCKS, D], BF16, name="wdown_sb")
-        nc.gpsimd.dma_start(wdown_sb[:], wdown.rearrange("(r p) c -> p r c", p=P))
+        nc.scalar.dma_start(wdown_sb[:], wdown.rearrange("(r p) c -> p r c", p=P))
 
         identity = held.tile([P, P], F32, name="identity")
         make_identity(nc, identity[:])

@@ -15,8 +15,11 @@ BLOCKS = S // P
 CHUNK = 4
 CHUNKS = BLOCKS // CHUNK
 M_BLOCKS = M // P
+LINE = 8
 
 ROW_GAIN, ROW_BUP, ROW_BDOWN = 0, 1, 1 + M_BLOCKS
+
+SCALAR_SQUARES_CHUNK = 1
 
 
 def tile_transformerblock_kernel(tc, x, gain, wup, bup, wdown, bdown, offs, out):
@@ -24,8 +27,7 @@ def tile_transformerblock_kernel(tc, x, gain, wup, bup, wdown, bdown, offs, out)
     with (
         tc.tile_pool(name="held", bufs=1) as held,
         tc.tile_pool(name="squares", bufs=2) as squares,
-        tc.psum_pool(name="flipped", bufs=2) as flipped,
-        tc.psum_pool(name="hidden", bufs=4) as hidden,
+        tc.psum_pool(name="banks", bufs=CHUNKS) as banks,
         tc.psum_pool(name="single", bufs=1) as single,
     ):
         offsets = held.tile([P, N // 16], U16, name="offsets")
@@ -55,6 +57,31 @@ def tile_transformerblock_kernel(tc, x, gain, wup, bup, wdown, bdown, offs, out)
         eps = held.tile([P, 1], F32, name="eps")
         nc.vector.memset(eps[:], EPS)
 
+        warm_sqrt = held.tile([P, 1], F32, name="warm_sqrt")
+        nc.scalar.activation(warm_sqrt[:], eps[:], FUNC.Sqrt)
+
+        sumsq = held.tile([P, CHUNKS, LINE], F32, name="sumsq")
+        for c in range(CHUNKS):
+            for k in range(CHUNK):
+                x_block = x_chunks[c][:, k, :]
+                total = sumsq[:, c, k : k + 1]
+                if c == SCALAR_SQUARES_CHUNK:
+                    sq_scalar = squares.tile([P, D], F32, name="sq_scalar")
+                    nc.scalar.activation(sq_scalar[:], x_block, FUNC.Square, accum_out=total)
+                else:
+                    sq_vector = squares.tile([P, D], F32, name="sq_vector")
+                    nc.vector.scalar_tensor_tensor(
+                        sq_vector[:], x_block, 1.0, x_block, ALU.mult, ALU.mult, accum_out=total
+                    )
+
+        rms = held.tile([P, CHUNKS, CHUNK], F32, name="rms")
+        nc.scalar.activation(rms[:], sumsq[:, :, 0:CHUNK], FUNC.Sqrt, bias=eps[:], scale=1.0 / STREAM_WIDTH)
+        rstd = held.tile([P, CHUNKS, CHUNK], F32, name="rstd")
+        nc.vector.reciprocal(rstd[:], rms[:])
+
+        warm_gelu = held.tile([P, 1], F32, name="warm_gelu")
+        nc.scalar.activation(warm_gelu[:], rms[:, 0, 0:1], FUNC.Gelu)
+
         columns_ps = single.tile([P, P], F32, name="columns_ps")
         nc.tensor.transpose(columns_ps[:], rows[:], identity[:])
         columns = held.tile([P, ROW_BDOWN + 1], F32, name="columns")
@@ -62,51 +89,36 @@ def tile_transformerblock_kernel(tc, x, gain, wup, bup, wdown, bdown, offs, out)
         gain_col = columns[:, ROW_GAIN : ROW_GAIN + 1]
         bdown_col = columns[:, ROW_BDOWN : ROW_BDOWN + 1]
 
-        sumsq = held.tile([P, 2, BLOCKS // 2], F32, name="sumsq")
-        for b in range(BLOCKS):
-            x_block = x_chunks[b // CHUNK][:, b % CHUNK, :]
-            total = sumsq[:, b % 2, b // 2 : b // 2 + 1]
-            if b % 2 == 0:
-                sq_scalar = squares.tile([P, D], F32, name="sq_scalar")
-                nc.scalar.activation(sq_scalar[:], x_block, FUNC.Square, accum_out=total)
-            else:
-                sq_vector = squares.tile([P, D], F32, name="sq_vector")
-                nc.vector.scalar_tensor_tensor(
-                    sq_vector[:], x_block, 1.0, x_block, ALU.mult, ALU.mult, accum_out=total
-                )
-
-        rms = held.tile([P, 2, BLOCKS // 2], F32, name="rms")
-        nc.scalar.activation(rms[:], sumsq[:], FUNC.Sqrt, bias=eps[:], scale=1.0 / STREAM_WIDTH)
-        rstd = held.tile([P, 2, BLOCKS // 2], F32, name="rstd")
-        nc.vector.reciprocal(rstd[:], rms[:])
+        flipped_chunks = []
+        for c in range(CHUNKS):
+            scaled = held.tile([P, CHUNK, D], F32, name=f"scaled{c}")
+            flipped_ps = banks.tile([D, CHUNK * P], F32, name="flipped_ps", tag="bank")
+            for k in range(CHUNK):
+                nc.vector.tensor_scalar(scaled[:, k, :], x_chunks[c][:, k, :], rstd[:, c, k : k + 1], None, ALU.mult)
+                nc.tensor.transpose(flipped_ps[:, k * P : (k + 1) * P], scaled[:, k, :], identity[:])
+            flipped_chunks.append(flipped_ps)
 
         table = held.tile([D, S], BF16, name="table")
         for c in range(CHUNKS):
-            scaled = held.tile([P, CHUNK, D], F32, name=f"scaled{c}")
-            flipped_ps = flipped.tile([D, CHUNK * P], F32, name="flipped_ps")
-            for k in range(CHUNK):
-                b = c * CHUNK + k
-                rstd_col = rstd[:, b % 2, b // 2 : b // 2 + 1]
-                if b % 2 == 0:
-                    nc.scalar.activation(scaled[:, k, :], x_chunks[c][:, k, :], FUNC.Copy, scale=rstd_col)
-                else:
-                    nc.vector.tensor_scalar(scaled[:, k, :], x_chunks[c][:, k, :], rstd_col, None, ALU.mult)
-                nc.tensor.transpose(flipped_ps[:, k * P : (k + 1) * P], scaled[:, k, :], identity[:])
             table_part = table[:, c * CHUNK * P : (c + 1) * CHUNK * P]
-            if c % 2 == 0:
-                nc.vector.tensor_scalar(table_part, flipped_ps[:], gain_col, None, ALU.mult)
+            if c < CHUNKS // 2:
+                nc.vector.tensor_scalar(table_part, flipped_chunks[c][:], gain_col, None, ALU.mult)
             else:
-                nc.scalar.activation(table_part, flipped_ps[:], FUNC.Copy, scale=gain_col)
+                nc.scalar.activation(table_part, flipped_chunks[c][:], FUNC.Copy, scale=gain_col)
+
+        v_blocks = []
+        for r in range(M_BLOCKS):
+            v_ps = banks.tile([P, N], F32, name="v_ps", tag="bank")
+            nc.tensor.matmul(
+                v_ps[:], wup_sb[:, r * P : (r + 1) * P], table[:].indirect(offsets[:]), start=True, stop=True
+            )
+            v_blocks.append(v_ps)
 
         out_ps = single.tile([D, N], F32, name="out_ps")
         u = held.tile([P, M_BLOCKS, N], BF16, name="u")
         for r in range(M_BLOCKS):
-            v_ps = hidden.tile([P, N], F32, name="v_ps")
-            nc.tensor.matmul(
-                v_ps[:], wup_sb[:, r * P : (r + 1) * P], table[:].indirect(offsets[:]), start=True, stop=True
-            )
             bup_col = columns[:, ROW_BUP + r : ROW_BUP + r + 1]
-            nc.scalar.activation(u[:, r, :], v_ps[:], FUNC.Gelu, bias=bup_col)
+            nc.scalar.activation(u[:, r, :], v_blocks[r][:], FUNC.Gelu, bias=bup_col)
             nc.tensor.matmul(out_ps[:], wdown_sb[:, r, :], u[:, r, :], start=(r == 0), stop=(r == M_BLOCKS - 1))
 
         result = held.tile([D, N], F32, name="result")

@@ -30,16 +30,16 @@ def tile_transformerblock_kernel(tc, x, gain, wup, bup, wdown, bdown, offs, out)
         tc.psum_pool(name="banks", bufs=CHUNKS) as banks,
         tc.psum_pool(name="single", bufs=1) as single,
     ):
-        offsets = held.tile([P, N // 16], U16, name="offsets")
-        nc.sync.dma_start(offsets[:], offs)
-
-        x_blocks = x.rearrange("(b p) d -> p b d", p=P)
+        x_view = x.rearrange("(c p k) d -> c p k d", p=P, k=CHUNK)
         x_chunks = []
         for c in range(CHUNKS):
             x_chunk = held.tile([P, CHUNK, D], BF16, name=f"x_chunk{c}")
             queue = nc.sync if c % 2 == 0 else nc.scalar
-            queue.dma_start(x_chunk[:], x_blocks[:, c * CHUNK : (c + 1) * CHUNK, :])
+            queue.dma_start(x_chunk[:], x_view[c])
             x_chunks.append(x_chunk)
+
+        offsets = held.tile([P, N // 16], U16, name="offsets")
+        nc.sync.dma_start(offsets[:], offs)
 
         rows = held.tile([P, P], F32, name="rows")
         nc.vector.memset(rows[:], 0.0)
@@ -100,11 +100,12 @@ def tile_transformerblock_kernel(tc, x, gain, wup, bup, wdown, bdown, offs, out)
 
         table = held.tile([D, S], BF16, name="table")
         for c in range(CHUNKS):
-            table_part = table[:, c * CHUNK * P : (c + 1) * CHUNK * P]
+            table_part = table[:, c * CHUNK * P : (c + 1) * CHUNK * P].rearrange("d (p k) -> d p k", k=CHUNK)
+            in_token_order = flipped_chunks[c][:].rearrange("d (k p) -> d p k", k=CHUNK)
             if c < CHUNKS // 2:
-                nc.vector.tensor_scalar(table_part, flipped_chunks[c][:], gain_col, None, ALU.mult)
+                nc.vector.tensor_scalar(table_part, in_token_order, gain_col, None, ALU.mult)
             else:
-                nc.scalar.activation(table_part, flipped_chunks[c][:], FUNC.Copy, scale=gain_col)
+                nc.scalar.activation(table_part, in_token_order, FUNC.Copy, scale=gain_col)
 
         v_blocks = []
         for r in range(M_BLOCKS):

@@ -14,18 +14,18 @@ ALU = mybir.AluOpType
 BLOCKS = S // P
 CHUNK = 4
 CHUNKS = BLOCKS // CHUNK
+HALF = CHUNK // 2
 M_BLOCKS = M // P
 LINE = 8
 
 ROW_GAIN, ROW_BUP, ROW_BDOWN = 0, 1, 1 + M_BLOCKS
-
-SCALAR_SQUARES_CHUNK = 1
 
 
 def tile_transformerblock_kernel(tc, x, gain, wup, bup, wdown, bdown, offs, out):
     nc = tc.nc
     with (
         tc.tile_pool(name="held", bufs=1) as held,
+        tc.tile_pool(name="per_chunk", bufs=CHUNKS) as per_chunk,
         tc.tile_pool(name="squares", bufs=2) as squares,
         tc.psum_pool(name="banks", bufs=CHUNKS) as banks,
         tc.psum_pool(name="single", bufs=1) as single,
@@ -33,7 +33,7 @@ def tile_transformerblock_kernel(tc, x, gain, wup, bup, wdown, bdown, offs, out)
         x_view = x.rearrange("(c p k) d -> c p k d", p=P, k=CHUNK)
         x_chunks = []
         for c in range(CHUNKS):
-            x_chunk = held.tile([P, CHUNK, D], BF16, name=f"x_chunk{c}")
+            x_chunk = per_chunk.tile([P, CHUNK, D], BF16, name="x_chunk")
             queue = nc.sync if c % 2 == 0 else nc.scalar
             queue.dma_start(x_chunk[:], x_view[c])
             x_chunks.append(x_chunk)
@@ -60,49 +60,55 @@ def tile_transformerblock_kernel(tc, x, gain, wup, bup, wdown, bdown, offs, out)
         warm_sqrt = held.tile([P, 1], F32, name="warm_sqrt")
         nc.scalar.activation(warm_sqrt[:], eps[:], FUNC.Sqrt)
 
-        sumsq = held.tile([P, CHUNKS, LINE], F32, name="sumsq")
-        for c in range(CHUNKS):
-            for k in range(CHUNK):
-                x_block = x_chunks[c][:, k, :]
-                total = sumsq[:, c, k : k + 1]
-                if c == SCALAR_SQUARES_CHUNK:
-                    sq_scalar = squares.tile([P, D], F32, name="sq_scalar")
-                    nc.scalar.activation(sq_scalar[:], x_block, FUNC.Square, accum_out=total)
-                else:
-                    sq_vector = squares.tile([P, D], F32, name="sq_vector")
-                    nc.vector.scalar_tensor_tensor(
-                        sq_vector[:], x_block, 1.0, x_block, ALU.mult, ALU.mult, accum_out=total
-                    )
+        rms_chunks, flipped_chunks = [], []
+        for step in range(CHUNKS + 1):
+            if step < CHUNKS:
+                x_chunk = x_chunks[step]
+                sumsq = per_chunk.tile([P, 2, LINE], F32, name="sumsq")
+                for k in range(CHUNK):
+                    total = sumsq[:, k // HALF, k % HALF : k % HALF + 1]
+                    if k < HALF:
+                        sq_vector = squares.tile([P, D], F32, name="sq_vector")
+                        nc.vector.scalar_tensor_tensor(
+                            sq_vector[:], x_chunk[:, k, :], 1.0, x_chunk[:, k, :], ALU.mult, ALU.mult, accum_out=total
+                        )
+                    else:
+                        sq_scalar = squares.tile([P, D], F32, name="sq_scalar")
+                        nc.scalar.activation(sq_scalar[:], x_chunk[:, k, :], FUNC.Square, accum_out=total)
+                rms = per_chunk.tile([P, 2, HALF], F32, name="rms")
+                nc.scalar.activation(rms[:], sumsq[:, :, 0:HALF], FUNC.Sqrt, bias=eps[:], scale=1.0 / STREAM_WIDTH)
+                rms_chunks.append(rms)
 
-        rms = held.tile([P, CHUNKS, CHUNK], F32, name="rms")
-        nc.scalar.activation(rms[:], sumsq[:, :, 0:CHUNK], FUNC.Sqrt, bias=eps[:], scale=1.0 / STREAM_WIDTH)
-        rstd = held.tile([P, CHUNKS, CHUNK], F32, name="rstd")
-        nc.vector.reciprocal(rstd[:], rms[:])
+            if step == CHUNKS - 1:
+                warm_gelu = held.tile([P, 1], F32, name="warm_gelu")
+                nc.scalar.activation(warm_gelu[:], rms_chunks[step][:, 0, 0:1], FUNC.Gelu)
 
-        warm_gelu = held.tile([P, 1], F32, name="warm_gelu")
-        nc.scalar.activation(warm_gelu[:], rms[:, 0, 0:1], FUNC.Gelu)
+            if step >= 1:
+                x_chunk = x_chunks[step - 1]
+                rstd = per_chunk.tile([P, 2, HALF], F32, name="rstd")
+                nc.vector.reciprocal(rstd[:], rms_chunks[step - 1][:])
+                scaled = per_chunk.tile([P, CHUNK, D], F32, name="scaled")
+                flipped_ps = banks.tile([D, CHUNK * P], F32, name="flipped_ps", tag="bank")
+                for k in range(CHUNK):
+                    rstd_col = rstd[:, k // HALF, k % HALF : k % HALF + 1]
+                    nc.vector.tensor_scalar(scaled[:, k, :], x_chunk[:, k, :], rstd_col, None, ALU.mult)
+                    nc.tensor.transpose(flipped_ps[:, k * P : (k + 1) * P], scaled[:, k, :], identity[:])
+                flipped_chunks.append(flipped_ps)
 
-        columns_ps = single.tile([P, P], F32, name="columns_ps")
-        nc.tensor.transpose(columns_ps[:], rows[:], identity[:])
+            if step == 1:
+                columns_ps = single.tile([P, P], F32, name="columns_ps")
+                nc.tensor.transpose(columns_ps[:], rows[:], identity[:])
+
         columns = held.tile([P, ROW_BDOWN + 1], F32, name="columns")
         nc.vector.tensor_copy(columns[:], columns_ps[:, 0 : ROW_BDOWN + 1])
         gain_col = columns[:, ROW_GAIN : ROW_GAIN + 1]
         bdown_col = columns[:, ROW_BDOWN : ROW_BDOWN + 1]
 
-        flipped_chunks = []
-        for c in range(CHUNKS):
-            scaled = held.tile([P, CHUNK, D], F32, name=f"scaled{c}")
-            flipped_ps = banks.tile([D, CHUNK * P], F32, name="flipped_ps", tag="bank")
-            for k in range(CHUNK):
-                nc.vector.tensor_scalar(scaled[:, k, :], x_chunks[c][:, k, :], rstd[:, c, k : k + 1], None, ALU.mult)
-                nc.tensor.transpose(flipped_ps[:, k * P : (k + 1) * P], scaled[:, k, :], identity[:])
-            flipped_chunks.append(flipped_ps)
-
         table = held.tile([D, S], BF16, name="table")
         for c in range(CHUNKS):
             table_part = table[:, c * CHUNK * P : (c + 1) * CHUNK * P].rearrange("d (p k) -> d p k", k=CHUNK)
             in_token_order = flipped_chunks[c][:].rearrange("d (k p) -> d p k", k=CHUNK)
-            if c < CHUNKS // 2:
+            if c < CHUNKS - 1:
                 nc.vector.tensor_scalar(table_part, in_token_order, gain_col, None, ALU.mult)
             else:
                 nc.scalar.activation(table_part, in_token_order, FUNC.Copy, scale=gain_col)

@@ -17,6 +17,8 @@ CHUNKS = BLOCKS // CHUNK
 HALF = CHUNK // 2
 M_BLOCKS = M // P
 LINE = 8
+WARM_MATMULS = 8
+N_HALF = N // 2
 
 ROW_GAIN, ROW_BUP, ROW_BDOWN = 0, 1, 1 + M_BLOCKS
 
@@ -56,6 +58,12 @@ def tile_transformerblock_kernel(tc, x, gain, wup, bup, wdown, bdown, offs, out)
         make_identity(nc, identity[:])
         eps = held.tile([P, 1], F32, name="eps")
         nc.vector.memset(eps[:], EPS)
+
+        zeros = held.tile([P, N], BF16, name="zeros")
+        nc.gpsimd.memset(zeros[:], 0.0)
+        idle_ps = single.tile([P, N], F32, name="idle_ps")
+        for i in range(WARM_MATMULS):
+            nc.tensor.matmul(idle_ps[:], zeros[:, 0:P], zeros[:], start=True, stop=True)
 
         warm_sqrt = held.tile([P, 1], F32, name="warm_sqrt")
         nc.scalar.activation(warm_sqrt[:], eps[:], FUNC.Sqrt)
@@ -121,13 +129,22 @@ def tile_transformerblock_kernel(tc, x, gain, wup, bup, wdown, bdown, offs, out)
             )
             v_blocks.append(v_ps)
 
-        out_ps = single.tile([D, N], F32, name="out_ps")
+        out_halves = [single.tile([D, N_HALF], F32, name=f"out_ps{i}") for i in range(2)]
         u = held.tile([P, M_BLOCKS, N], BF16, name="u")
         for r in range(M_BLOCKS):
             bup_col = columns[:, ROW_BUP + r : ROW_BUP + r + 1]
             nc.scalar.activation(u[:, r, :], v_blocks[r][:], FUNC.Gelu, bias=bup_col)
-            nc.tensor.matmul(out_ps[:], wdown_sb[:, r, :], u[:, r, :], start=(r == 0), stop=(r == M_BLOCKS - 1))
+            for i in range(2):
+                nc.tensor.matmul(
+                    out_halves[i][:],
+                    wdown_sb[:, r, :],
+                    u[:, r, i * N_HALF : (i + 1) * N_HALF],
+                    start=(r == 0),
+                    stop=(r == M_BLOCKS - 1),
+                )
 
         result = held.tile([D, N], F32, name="result")
-        nc.vector.tensor_scalar(result[:], out_ps[:], bdown_col, None, ALU.add)
-        nc.sync.dma_start(out, result[:])
+        nc.vector.tensor_scalar(result[:, 0:N_HALF], out_halves[0][:], bdown_col, None, ALU.add)
+        nc.sync.dma_start(out[:, 0:N_HALF], result[:, 0:N_HALF])
+        nc.scalar.activation(result[:, N_HALF:N], out_halves[1][:], FUNC.Identity, bias=bdown_col)
+        nc.scalar.dma_start(out[:, N_HALF:N], result[:, N_HALF:N])

@@ -17,7 +17,6 @@ CHUNKS = BLOCKS // CHUNK
 HALF = CHUNK // 2
 M_BLOCKS = M // P
 LINE = 8
-WARM_MATMULS = 8
 N_HALF = N // 2
 
 ROW_GAIN, ROW_BUP, ROW_BDOWN = 0, 1, 1 + M_BLOCKS
@@ -36,8 +35,7 @@ def tile_transformerblock_kernel(tc, x, gain, wup, bup, wdown, bdown, offs, out)
         x_chunks = []
         for c in range(CHUNKS):
             x_chunk = per_chunk.tile([P, CHUNK, D], BF16, name="x_chunk")
-            queue = nc.sync if c % 2 == 0 else nc.scalar
-            queue.dma_start(x_chunk[:], x_view[c])
+            nc.sync.dma_start(x_chunk[:], x_view[c])
             x_chunks.append(x_chunk)
 
         offsets = held.tile([P, N // 16], U16, name="offsets")
@@ -50,20 +48,14 @@ def tile_transformerblock_kernel(tc, x, gain, wup, bup, wdown, bdown, offs, out)
         nc.sync.dma_start(rows[ROW_BDOWN : ROW_BDOWN + 1, :], bdown.rearrange("d o -> o d"))
 
         wup_sb = held.tile([D, M], BF16, name="wup_sb")
-        nc.scalar.dma_start(wup_sb[:], wup)
+        nc.sync.dma_start(wup_sb[:], wup)
         wdown_sb = held.tile([P, M_BLOCKS, D], BF16, name="wdown_sb")
-        nc.scalar.dma_start(wdown_sb[:], wdown.rearrange("(r p) c -> p r c", p=P))
+        nc.sync.dma_start(wdown_sb[:], wdown.rearrange("(r p) c -> p r c", p=P))
 
         identity = held.tile([P, P], F32, name="identity")
         make_identity(nc, identity[:])
         eps = held.tile([P, 1], F32, name="eps")
         nc.vector.memset(eps[:], EPS)
-
-        zeros = held.tile([P, N], BF16, name="zeros")
-        nc.gpsimd.memset(zeros[:], 0.0)
-        idle_ps = single.tile([P, N], F32, name="idle_ps")
-        for i in range(WARM_MATMULS):
-            nc.tensor.matmul(idle_ps[:], zeros[:, 0:P], zeros[:], start=True, stop=True)
 
         warm_sqrt = held.tile([P, 1], F32, name="warm_sqrt")
         nc.scalar.activation(warm_sqrt[:], eps[:], FUNC.Sqrt)

@@ -108,10 +108,7 @@ def tile_transformerblock_kernel(tc, x, gain, wup, bup, wdown, bdown, offs, out)
         for c in range(CHUNKS):
             table_part = table[:, c * CHUNK * P : (c + 1) * CHUNK * P].rearrange("d (p k) -> d p k", k=CHUNK)
             in_token_order = flipped_chunks[c][:].rearrange("d (k p) -> d p k", k=CHUNK)
-            if c < CHUNKS - 1:
-                nc.vector.tensor_scalar(table_part, in_token_order, gain_col, None, ALU.mult)
-            else:
-                nc.scalar.activation(table_part, in_token_order, FUNC.Copy, scale=gain_col)
+            nc.vector.tensor_scalar(table_part, in_token_order, gain_col, None, ALU.mult)
 
         v_blocks = []
         for r in range(M_BLOCKS):

@@ -57,10 +57,10 @@ def tile_transformerblock_kernel(tc, x, gain, wup, bup, wdown, bdown, offs, out)
         eps = held.tile([P, 1], F32, name="eps")
         nc.vector.memset(eps[:], EPS)
 
-        warm_sqrt = held.tile([P, 1], F32, name="warm_sqrt")
-        nc.scalar.activation(warm_sqrt[:], eps[:], FUNC.Sqrt)
+        warm_rsqrt = held.tile([P, 1], F32, name="warm_rsqrt")
+        nc.scalar.activation(warm_rsqrt[:], eps[:], FUNC.Abs_reciprocal_sqrt)
 
-        rms_chunks, flipped_chunks = [], []
+        rstd_chunks, flipped_chunks = [], []
         for step in range(CHUNKS + 1):
             if step < CHUNKS:
                 x_chunk = x_chunks[step]
@@ -75,18 +75,19 @@ def tile_transformerblock_kernel(tc, x, gain, wup, bup, wdown, bdown, offs, out)
                     else:
                         sq_scalar = squares.tile([P, D], F32, name="sq_scalar")
                         nc.scalar.activation(sq_scalar[:], x_chunk[:, k, :], FUNC.Square, accum_out=total)
-                rms = per_chunk.tile([P, 2, HALF], F32, name="rms")
-                nc.scalar.activation(rms[:], sumsq[:, :, 0:HALF], FUNC.Sqrt, bias=eps[:], scale=1.0 / STREAM_WIDTH)
-                rms_chunks.append(rms)
+                rstd = per_chunk.tile([P, 2, HALF], F32, name="rstd")
+                nc.scalar.activation(
+                    rstd[:], sumsq[:, :, 0:HALF], FUNC.Abs_reciprocal_sqrt, bias=eps[:], scale=1.0 / STREAM_WIDTH
+                )
+                rstd_chunks.append(rstd)
 
             if step == CHUNKS - 1:
                 warm_gelu = held.tile([P, 1], F32, name="warm_gelu")
-                nc.scalar.activation(warm_gelu[:], rms_chunks[step][:, 0, 0:1], FUNC.Gelu)
+                nc.scalar.activation(warm_gelu[:], rstd_chunks[step][:, 0, 0:1], FUNC.Gelu)
 
             if step >= 1:
                 x_chunk = x_chunks[step - 1]
-                rstd = per_chunk.tile([P, 2, HALF], F32, name="rstd")
-                nc.vector.reciprocal(rstd[:], rms_chunks[step - 1][:])
+                rstd = rstd_chunks[step - 1]
                 scaled = per_chunk.tile([P, CHUNK, D], F32, name="scaled")
                 flipped_ps = banks.tile([D, CHUNK * P], F32, name="flipped_ps", tag="bank")
                 for k in range(CHUNK):

@@ -60,8 +60,12 @@ def tile_transformerblock_kernel(tc, x, gain, wup, bup, wdown, bdown, offs, out)
         warm_rsqrt = held.tile([P, 1], F32, name="warm_rsqrt")
         nc.scalar.activation(warm_rsqrt[:], eps[:], FUNC.Abs_reciprocal_sqrt)
 
+        table = held.tile([D, S], BF16, name="table")
+        columns = held.tile([P, ROW_BDOWN + 1], F32, name="columns")
+        gain_col = columns[:, ROW_GAIN : ROW_GAIN + 1]
+        bdown_col = columns[:, ROW_BDOWN : ROW_BDOWN + 1]
         rstd_chunks, flipped_chunks = [], []
-        for step in range(CHUNKS + 1):
+        for step in range(CHUNKS + 2):
             if step < CHUNKS:
                 x_chunk = x_chunks[step]
                 sumsq = per_chunk.tile([P, 2, LINE], F32, name="sumsq")
@@ -81,11 +85,7 @@ def tile_transformerblock_kernel(tc, x, gain, wup, bup, wdown, bdown, offs, out)
                 )
                 rstd_chunks.append(rstd)
 
-            if step == CHUNKS - 1:
-                warm_gelu = held.tile([P, 1], F32, name="warm_gelu")
-                nc.scalar.activation(warm_gelu[:], rstd_chunks[step][:, 0, 0:1], FUNC.Gelu)
-
-            if step >= 1:
+            if 1 <= step <= CHUNKS:
                 x_chunk = x_chunks[step - 1]
                 rstd = rstd_chunks[step - 1]
                 scaled = per_chunk.tile([P, CHUNK, D], F32, name="scaled")
@@ -99,17 +99,19 @@ def tile_transformerblock_kernel(tc, x, gain, wup, bup, wdown, bdown, offs, out)
             if step == 1:
                 columns_ps = single.tile([P, P], F32, name="columns_ps")
                 nc.tensor.transpose(columns_ps[:], rows[:], identity[:])
+                nc.vector.tensor_copy(columns[:], columns_ps[:, 0 : ROW_BDOWN + 1])
 
-        columns = held.tile([P, ROW_BDOWN + 1], F32, name="columns")
-        nc.vector.tensor_copy(columns[:], columns_ps[:, 0 : ROW_BDOWN + 1])
-        gain_col = columns[:, ROW_GAIN : ROW_GAIN + 1]
-        bdown_col = columns[:, ROW_BDOWN : ROW_BDOWN + 1]
+            if step >= 2:
+                c = step - 2
+                table_part = table[:, c * CHUNK * P : (c + 1) * CHUNK * P].rearrange("d (p k) -> d p k", k=CHUNK)
+                in_token_order = flipped_chunks[c][:].rearrange("d (k p) -> d p k", k=CHUNK)
+                if 0 < c < CHUNKS - 1:
+                    nc.scalar.activation(table_part, in_token_order, FUNC.Copy, scale=gain_col)
+                else:
+                    nc.vector.tensor_scalar(table_part, in_token_order, gain_col, None, ALU.mult)
 
-        table = held.tile([D, S], BF16, name="table")
-        for c in range(CHUNKS):
-            table_part = table[:, c * CHUNK * P : (c + 1) * CHUNK * P].rearrange("d (p k) -> d p k", k=CHUNK)
-            in_token_order = flipped_chunks[c][:].rearrange("d (k p) -> d p k", k=CHUNK)
-            nc.vector.tensor_scalar(table_part, in_token_order, gain_col, None, ALU.mult)
+        warm_gelu = held.tile([P, 1], F32, name="warm_gelu")
+        nc.scalar.activation(warm_gelu[:], flipped_chunks[CHUNKS - 2][:, 0:1], FUNC.Gelu)
 
         v_blocks = []
         for r in range(M_BLOCKS):

@@ -19,8 +19,6 @@ M_BLOCKS = M // P
 LINE = 8
 N_HALF = N // 2
 
-ROW_GAIN, ROW_BUP, ROW_BDOWN = 0, 1, 1 + M_BLOCKS
-
 
 def tile_transformerblock_kernel(tc, x, gain, wup, bup, wdown, bdown, offs, out):
     nc = tc.nc
@@ -41,11 +39,12 @@ def tile_transformerblock_kernel(tc, x, gain, wup, bup, wdown, bdown, offs, out)
         offsets = held.tile([P, N // 16], U16, name="offsets")
         nc.sync.dma_start(offsets[:], offs)
 
-        rows = held.tile([P, P], F32, name="rows")
-        nc.vector.memset(rows[:], 0.0)
-        nc.sync.dma_start(rows[ROW_GAIN : ROW_GAIN + 1, :], gain.rearrange("d o -> o d"))
-        nc.sync.dma_start(rows[ROW_BUP : ROW_BUP + M_BLOCKS, :], bup.rearrange("(r p) o -> r (p o)", p=P))
-        nc.sync.dma_start(rows[ROW_BDOWN : ROW_BDOWN + 1, :], bdown.rearrange("d o -> o d"))
+        gain_col = held.tile([D, 1], F32, name="gain_col")
+        nc.sync.dma_start(gain_col[:], gain)
+        bup_cols = held.tile([P, M_BLOCKS], F32, name="bup_cols")
+        nc.sync.dma_start(bup_cols[:], bup.rearrange("(r p) o -> p (r o)", p=P))
+        bdown_col = held.tile([D, 1], F32, name="bdown_col")
+        nc.sync.dma_start(bdown_col[:], bdown)
 
         wup_sb = held.tile([D, M], BF16, name="wup_sb")
         nc.sync.dma_start(wup_sb[:], wup)
@@ -61,9 +60,6 @@ def tile_transformerblock_kernel(tc, x, gain, wup, bup, wdown, bdown, offs, out)
         nc.scalar.activation(warm_rsqrt[:], eps[:], FUNC.Abs_reciprocal_sqrt)
 
         table = held.tile([D, S], BF16, name="table")
-        columns = held.tile([P, ROW_BDOWN + 1], F32, name="columns")
-        gain_col = columns[:, ROW_GAIN : ROW_GAIN + 1]
-        bdown_col = columns[:, ROW_BDOWN : ROW_BDOWN + 1]
         rstd_chunks, flipped_chunks = [], []
         for step in range(CHUNKS + 2):
             if step < CHUNKS:
@@ -96,19 +92,14 @@ def tile_transformerblock_kernel(tc, x, gain, wup, bup, wdown, bdown, offs, out)
                     nc.tensor.transpose(flipped_ps[:, k * P : (k + 1) * P], scaled[:, k, :], identity[:])
                 flipped_chunks.append(flipped_ps)
 
-            if step == 1:
-                columns_ps = single.tile([P, P], F32, name="columns_ps")
-                nc.tensor.transpose(columns_ps[:], rows[:], identity[:])
-                nc.vector.tensor_copy(columns[:], columns_ps[:, 0 : ROW_BDOWN + 1])
-
             if step >= 2:
                 c = step - 2
                 table_part = table[:, c * CHUNK * P : (c + 1) * CHUNK * P].rearrange("d (p k) -> d p k", k=CHUNK)
                 in_token_order = flipped_chunks[c][:].rearrange("d (k p) -> d p k", k=CHUNK)
                 if 0 < c < CHUNKS - 1:
-                    nc.scalar.activation(table_part, in_token_order, FUNC.Copy, scale=gain_col)
+                    nc.scalar.activation(table_part, in_token_order, FUNC.Copy, scale=gain_col[:])
                 else:
-                    nc.vector.tensor_scalar(table_part, in_token_order, gain_col, None, ALU.mult)
+                    nc.vector.tensor_scalar(table_part, in_token_order, gain_col[:], None, ALU.mult)
 
         warm_gelu = held.tile([P, 1], F32, name="warm_gelu")
         nc.scalar.activation(warm_gelu[:], flipped_chunks[CHUNKS - 2][:, 0:1], FUNC.Gelu)
@@ -124,8 +115,7 @@ def tile_transformerblock_kernel(tc, x, gain, wup, bup, wdown, bdown, offs, out)
         out_halves = [single.tile([D, N_HALF], F32, name=f"out_ps{i}") for i in range(2)]
         u = held.tile([P, M_BLOCKS, N], BF16, name="u")
         for r in range(M_BLOCKS):
-            bup_col = columns[:, ROW_BUP + r : ROW_BUP + r + 1]
-            nc.scalar.activation(u[:, r, :], v_blocks[r][:], FUNC.Gelu, bias=bup_col)
+            nc.scalar.activation(u[:, r, :], v_blocks[r][:], FUNC.Gelu, bias=bup_cols[:, r : r + 1])
             for i in range(2):
                 nc.tensor.matmul(
                     out_halves[i][:],
@@ -136,7 +126,7 @@ def tile_transformerblock_kernel(tc, x, gain, wup, bup, wdown, bdown, offs, out)
                 )
 
         result = held.tile([D, N], F32, name="result")
-        nc.vector.tensor_scalar(result[:, 0:N_HALF], out_halves[0][:], bdown_col, None, ALU.add)
+        nc.vector.tensor_scalar(result[:, 0:N_HALF], out_halves[0][:], bdown_col[:], None, ALU.add)
         nc.sync.dma_start(out[:, 0:N_HALF], result[:, 0:N_HALF])
-        nc.scalar.activation(result[:, N_HALF:N], out_halves[1][:], FUNC.Identity, bias=bdown_col)
+        nc.scalar.activation(result[:, N_HALF:N], out_halves[1][:], FUNC.Identity, bias=bdown_col[:])
         nc.scalar.dma_start(out[:, N_HALF:N], result[:, N_HALF:N])

@@ -26,7 +26,7 @@ def tile_transformerblock_kernel(tc, x, gain, wup, bup, wdown, bdown, offs, out)
         tc.tile_pool(name="held", bufs=1) as held,
         tc.tile_pool(name="per_chunk", bufs=CHUNKS) as per_chunk,
         tc.tile_pool(name="squares", bufs=2) as squares,
-        tc.psum_pool(name="banks", bufs=CHUNKS) as banks,
+        tc.psum_pool(name="banks", bufs=M_BLOCKS + 1) as banks,
         tc.psum_pool(name="single", bufs=1) as single,
     ):
         x_view = x.rearrange("(c p k) d -> c p k d", p=P, k=CHUNK)
@@ -104,18 +104,30 @@ def tile_transformerblock_kernel(tc, x, gain, wup, bup, wdown, bdown, offs, out)
         warm_gelu = held.tile([P, 1], F32, name="warm_gelu")
         nc.scalar.activation(warm_gelu[:], flipped_chunks[CHUNKS - 2][:, 0:1], FUNC.Gelu)
 
-        v_blocks = []
+        v_pieces = []
         for r in range(M_BLOCKS):
-            v_ps = banks.tile([P, N], F32, name="v_ps", tag="bank")
-            nc.tensor.matmul(
-                v_ps[:], wup_sb[:, r * P : (r + 1) * P], table[:].indirect(offsets[:]), start=True, stop=True
-            )
-            v_blocks.append(v_ps)
+            wup_block = wup_sb[:, r * P : (r + 1) * P]
+            if r == 0:
+                pieces = []
+                for i in range(2):
+                    v_ps = banks.tile([P, N_HALF], F32, name="v_ps", tag="bank")
+                    half_of_list = offsets[:, i * N_HALF // 16 : (i + 1) * N_HALF // 16]
+                    nc.tensor.matmul(v_ps[:], wup_block, table[:].indirect(half_of_list), start=True, stop=True)
+                    pieces.append((i * N_HALF, N_HALF, v_ps[:]))
+            else:
+                v_ps = banks.tile([P, N], F32, name="v_ps", tag="bank")
+                nc.tensor.matmul(v_ps[:], wup_block, table[:].indirect(offsets[:]), start=True, stop=True)
+                if r == M_BLOCKS - 1:
+                    pieces = [(i * N_HALF, N_HALF, v_ps[:, i * N_HALF : (i + 1) * N_HALF]) for i in range(2)]
+                else:
+                    pieces = [(0, N, v_ps[:])]
+            v_pieces.append(pieces)
 
         out_halves = [single.tile([D, N_HALF], F32, name=f"out_ps{i}") for i in range(2)]
         u = held.tile([P, M_BLOCKS, N], BF16, name="u")
         for r in range(M_BLOCKS):
-            nc.scalar.activation(u[:, r, :], v_blocks[r][:], FUNC.Gelu, bias=bup_cols[:, r : r + 1])
+            for first, tokens, v_piece in v_pieces[r]:
+                nc.scalar.activation(u[:, r, first : first + tokens], v_piece, FUNC.Gelu, bias=bup_cols[:, r : r + 1])
             for i in range(2):
                 nc.tensor.matmul(
                     out_halves[i][:],
@@ -126,7 +138,7 @@ def tile_transformerblock_kernel(tc, x, gain, wup, bup, wdown, bdown, offs, out)
                 )
 
         result = held.tile([D, N], F32, name="result")
-        nc.vector.tensor_scalar(result[:, 0:N_HALF], out_halves[0][:], bdown_col[:], None, ALU.add)
-        nc.sync.dma_start(out[:, 0:N_HALF], result[:, 0:N_HALF])
-        nc.scalar.activation(result[:, N_HALF:N], out_halves[1][:], FUNC.Identity, bias=bdown_col[:])
-        nc.scalar.dma_start(out[:, N_HALF:N], result[:, N_HALF:N])
+        for i in range(2):
+            half = slice(i * N_HALF, (i + 1) * N_HALF)
+            nc.vector.tensor_scalar(result[:, half], out_halves[i][:], bdown_col[:], None, ALU.add)
+            nc.sync.dma_start(out[:, half], result[:, half])

@@ -11,12 +11,12 @@ BF16, F32, U16 = mybir.dt.bfloat16, mybir.dt.float32, mybir.dt.uint16
 FUNC = mybir.ActivationFunctionType
 ALU = mybir.AluOpType
 
-BLOCKS = S // P
-CHUNK = 4
-CHUNKS = BLOCKS // CHUNK
-HALF = CHUNK // 2
+CHUNK_BLOCKS = (4, 4, 4, 2, 2)
+CHUNKS = len(CHUNK_BLOCKS)
+FIRST_TOKEN = [P * sum(CHUNK_BLOCKS[:c]) for c in range(CHUNKS)]
+assert P * sum(CHUNK_BLOCKS) == S
+SCALAR_COPIES = (1, 2)
 M_BLOCKS = M // P
-LINE = 8
 N_HALF = N // 2
 
 
@@ -26,14 +26,15 @@ def tile_transformerblock_kernel(tc, x, gain, wup, bup, wdown, bdown, offs, out)
         tc.tile_pool(name="held", bufs=1) as held,
         tc.tile_pool(name="per_chunk", bufs=CHUNKS) as per_chunk,
         tc.tile_pool(name="squares", bufs=2) as squares,
-        tc.psum_pool(name="banks", bufs=M_BLOCKS + 1) as banks,
+        tc.psum_pool(name="banks", bufs=CHUNKS) as banks,
         tc.psum_pool(name="single", bufs=1) as single,
     ):
-        x_view = x.rearrange("(c p k) d -> c p k d", p=P, k=CHUNK)
         x_chunks = []
         for c in range(CHUNKS):
-            x_chunk = per_chunk.tile([P, CHUNK, D], BF16, name="x_chunk")
-            nc.sync.dma_start(x_chunk[:], x_view[c])
+            blocks = CHUNK_BLOCKS[c]
+            x_chunk = per_chunk.tile([P, blocks, D], BF16, name="x_chunk")
+            rows_of_x = x[FIRST_TOKEN[c] : FIRST_TOKEN[c] + blocks * P, :]
+            nc.sync.dma_start(x_chunk[:], rows_of_x.rearrange("(p k) d -> p k d", k=blocks))
             x_chunks.append(x_chunk)
 
         offsets = held.tile([P, N // 16], U16, name="offsets")
@@ -64,10 +65,11 @@ def tile_transformerblock_kernel(tc, x, gain, wup, bup, wdown, bdown, offs, out)
         for step in range(CHUNKS + 2):
             if step < CHUNKS:
                 x_chunk = x_chunks[step]
-                sumsq = per_chunk.tile([P, 2, LINE], F32, name="sumsq")
-                for k in range(CHUNK):
-                    total = sumsq[:, k // HALF, k % HALF : k % HALF + 1]
-                    if k < HALF:
+                blocks = CHUNK_BLOCKS[step]
+                sumsq = per_chunk.tile([P, blocks], F32, name="sumsq")
+                for k in range(blocks):
+                    total = sumsq[:, k : k + 1]
+                    if k < blocks // 2:
                         sq_vector = squares.tile([P, D], F32, name="sq_vector")
                         nc.vector.scalar_tensor_tensor(
                             sq_vector[:], x_chunk[:, k, :], 1.0, x_chunk[:, k, :], ALU.mult, ALU.mult, accum_out=total
@@ -75,34 +77,35 @@ def tile_transformerblock_kernel(tc, x, gain, wup, bup, wdown, bdown, offs, out)
                     else:
                         sq_scalar = squares.tile([P, D], F32, name="sq_scalar")
                         nc.scalar.activation(sq_scalar[:], x_chunk[:, k, :], FUNC.Square, accum_out=total)
-                rstd = per_chunk.tile([P, 2, HALF], F32, name="rstd")
+                rstd = per_chunk.tile([P, blocks], F32, name="rstd")
                 nc.scalar.activation(
-                    rstd[:], sumsq[:, :, 0:HALF], FUNC.Abs_reciprocal_sqrt, bias=eps[:], scale=1.0 / STREAM_WIDTH
+                    rstd[:], sumsq[:], FUNC.Abs_reciprocal_sqrt, bias=eps[:], scale=1.0 / STREAM_WIDTH
                 )
                 rstd_chunks.append(rstd)
 
             if 1 <= step <= CHUNKS:
                 x_chunk = x_chunks[step - 1]
                 rstd = rstd_chunks[step - 1]
-                scaled = per_chunk.tile([P, CHUNK, D], F32, name="scaled")
-                flipped_ps = banks.tile([D, CHUNK * P], F32, name="flipped_ps", tag="bank")
-                for k in range(CHUNK):
-                    rstd_col = rstd[:, k // HALF, k % HALF : k % HALF + 1]
-                    nc.vector.tensor_scalar(scaled[:, k, :], x_chunk[:, k, :], rstd_col, None, ALU.mult)
+                blocks = CHUNK_BLOCKS[step - 1]
+                scaled = per_chunk.tile([P, blocks, D], F32, name="scaled")
+                flipped_ps = banks.tile([D, blocks * P], F32, name="flipped_ps", tag="bank")
+                for k in range(blocks):
+                    nc.vector.tensor_scalar(scaled[:, k, :], x_chunk[:, k, :], rstd[:, k : k + 1], None, ALU.mult)
                     nc.tensor.transpose(flipped_ps[:, k * P : (k + 1) * P], scaled[:, k, :], identity[:])
                 flipped_chunks.append(flipped_ps)
 
             if step >= 2:
                 c = step - 2
-                table_part = table[:, c * CHUNK * P : (c + 1) * CHUNK * P].rearrange("d (p k) -> d p k", k=CHUNK)
-                in_token_order = flipped_chunks[c][:].rearrange("d (k p) -> d p k", k=CHUNK)
-                if 0 < c < CHUNKS - 1:
+                blocks = CHUNK_BLOCKS[c]
+                table_part = table[:, FIRST_TOKEN[c] : FIRST_TOKEN[c] + blocks * P].rearrange("d (p k) -> d p k", k=blocks)
+                in_token_order = flipped_chunks[c][:].rearrange("d (k p) -> d p k", k=blocks)
+                if c in SCALAR_COPIES:
                     nc.scalar.activation(table_part, in_token_order, FUNC.Copy, scale=gain_col[:])
                 else:
                     nc.vector.tensor_scalar(table_part, in_token_order, gain_col[:], None, ALU.mult)
 
         warm_gelu = held.tile([P, 1], F32, name="warm_gelu")
-        nc.scalar.activation(warm_gelu[:], flipped_chunks[CHUNKS - 2][:, 0:1], FUNC.Gelu)
+        nc.scalar.activation(warm_gelu[:], flipped_chunks[SCALAR_COPIES[-1]][:, 0:1], FUNC.Gelu)
 
         v_pieces = []
         for r in range(M_BLOCKS):

@@ -18,6 +18,7 @@ assert P * sum(CHUNK_BLOCKS) == S
 SCALAR_COPIES = (1, 2)
 M_BLOCKS = M // P
 N_HALF = N // 2
+STORES = ((0, N // 2), (N // 2, N // 4), (3 * N // 4, N // 4))
 
 
 def tile_transformerblock_kernel(tc, x, gain, wup, bup, wdown, bdown, offs, out):
@@ -144,4 +145,5 @@ def tile_transformerblock_kernel(tc, x, gain, wup, bup, wdown, bdown, offs, out)
         for i in range(2):
             half = slice(i * N_HALF, (i + 1) * N_HALF)
             nc.vector.tensor_scalar(result[:, half], out_halves[i][:], bdown_col[:], None, ALU.add)
-            nc.sync.dma_start(out[:, half], result[:, half])
+        for first, tokens in STORES:
+            nc.sync.dma_start(out[:, first : first + tokens], result[:, first : first + tokens])

@@ -70,7 +70,7 @@ def tile_transformerblock_kernel(tc, x, gain, wup, bup, wdown, bdown, offs, out)
                 sumsq = per_chunk.tile([P, blocks], F32, name="sumsq")
                 for k in range(blocks):
                     total = sumsq[:, k : k + 1]
-                    if k < blocks // 2:
+                    if k % 2 == 0 and step < CHUNKS - 2:
                         sq_vector = squares.tile([P, D], F32, name="sq_vector")
                         nc.vector.scalar_tensor_tensor(
                             sq_vector[:], x_chunk[:, k, :], 1.0, x_chunk[:, k, :], ALU.mult, ALU.mult, accum_out=total
@@ -79,9 +79,15 @@ def tile_transformerblock_kernel(tc, x, gain, wup, bup, wdown, bdown, offs, out)
                         sq_scalar = squares.tile([P, D], F32, name="sq_scalar")
                         nc.scalar.activation(sq_scalar[:], x_chunk[:, k, :], FUNC.Square, accum_out=total)
                 rstd = per_chunk.tile([P, blocks], F32, name="rstd")
-                nc.scalar.activation(
-                    rstd[:], sumsq[:], FUNC.Abs_reciprocal_sqrt, bias=eps[:], scale=1.0 / STREAM_WIDTH
-                )
+                group = 2 if step == 0 else blocks
+                for k in range(0, blocks, group):
+                    nc.scalar.activation(
+                        rstd[:, k : k + group],
+                        sumsq[:, k : k + group],
+                        FUNC.Abs_reciprocal_sqrt,
+                        bias=eps[:],
+                        scale=1.0 / STREAM_WIDTH,
+                    )
                 rstd_chunks.append(rstd)
 
             if 1 <= step <= CHUNKS:

import concourse.mybir as mybir
from concourse.masks import make_identity

S, D, M, N = 2048, 128, 512, 512
P = 128
STREAM_WIDTH = 256
EPS = 1e-6
FLOPS = 2 * D * M * N + 2 * M * D * N

BF16, F32, U16 = mybir.dt.bfloat16, mybir.dt.float32, mybir.dt.uint16
FUNC = mybir.ActivationFunctionType
ALU = mybir.AluOpType

CHUNK_BLOCKS = (4, 4, 4, 2, 2)
CHUNKS = len(CHUNK_BLOCKS)
FIRST_TOKEN = [P * sum(CHUNK_BLOCKS[:c]) for c in range(CHUNKS)]
assert P * sum(CHUNK_BLOCKS) == S
SCALAR_COPIES = (1, 2)
M_BLOCKS = M // P
N_HALF = N // 2
STORES = ((0, N // 2), (N // 2, N // 4), (3 * N // 4, N // 4))


def tile_transformerblock_kernel(tc, x, gain, wup, bup, wdown, bdown, offs, out):
    nc = tc.nc
    with (
        tc.tile_pool(name="held", bufs=1) as held,
        tc.tile_pool(name="per_chunk", bufs=CHUNKS) as per_chunk,
        tc.tile_pool(name="squares", bufs=2) as squares,
        tc.psum_pool(name="banks", bufs=CHUNKS) as banks,
        tc.psum_pool(name="single", bufs=1) as single,
    ):
        x_chunks = []
        for c in range(CHUNKS):
            blocks = CHUNK_BLOCKS[c]
            x_chunk = per_chunk.tile([P, blocks, D], BF16, name="x_chunk")
            rows_of_x = x[FIRST_TOKEN[c] : FIRST_TOKEN[c] + blocks * P, :]
            nc.sync.dma_start(x_chunk[:], rows_of_x.rearrange("(p k) d -> p k d", k=blocks))
            x_chunks.append(x_chunk)

        offsets = held.tile([P, N // 16], U16, name="offsets")
        nc.sync.dma_start(offsets[:], offs)

        gain_col = held.tile([D, 1], F32, name="gain_col")
        nc.sync.dma_start(gain_col[:], gain)
        bup_cols = held.tile([P, M_BLOCKS], F32, name="bup_cols")
        nc.sync.dma_start(bup_cols[:], bup.rearrange("(r p) o -> p (r o)", p=P))
        bdown_col = held.tile([D, 1], F32, name="bdown_col")
        nc.sync.dma_start(bdown_col[:], bdown)

        wup_sb = held.tile([D, M], BF16, name="wup_sb")
        nc.sync.dma_start(wup_sb[:], wup)
        wdown_sb = held.tile([P, M_BLOCKS, D], BF16, name="wdown_sb")
        nc.sync.dma_start(wdown_sb[:], wdown.rearrange("(r p) c -> p r c", p=P))

        identity = held.tile([P, P], F32, name="identity")
        make_identity(nc, identity[:])
        eps = held.tile([P, 1], F32, name="eps")
        nc.vector.memset(eps[:], EPS)

        warm_rsqrt = held.tile([P, 1], F32, name="warm_rsqrt")
        nc.scalar.activation(warm_rsqrt[:], eps[:], FUNC.Abs_reciprocal_sqrt)

        table = held.tile([D, S], BF16, name="table")
        rstd_chunks, flipped_chunks = [], []
        for step in range(CHUNKS + 2):
            if step < CHUNKS:
                x_chunk = x_chunks[step]
                blocks = CHUNK_BLOCKS[step]
                sumsq = per_chunk.tile([P, blocks], F32, name="sumsq")
                for k in range(blocks):
                    total = sumsq[:, k : k + 1]
                    if k % 2 == 0 and step < CHUNKS - 2:
                        sq_vector = squares.tile([P, D], F32, name="sq_vector")
                        nc.vector.scalar_tensor_tensor(
                            sq_vector[:], x_chunk[:, k, :], 1.0, x_chunk[:, k, :], ALU.mult, ALU.mult, accum_out=total
                        )
                    else:
                        sq_scalar = squares.tile([P, D], F32, name="sq_scalar")
                        nc.scalar.activation(sq_scalar[:], x_chunk[:, k, :], FUNC.Square, accum_out=total)
                rstd = per_chunk.tile([P, blocks], F32, name="rstd")
                group = 2 if step == 0 else blocks
                for k in range(0, blocks, group):
                    nc.scalar.activation(
                        rstd[:, k : k + group],
                        sumsq[:, k : k + group],
                        FUNC.Abs_reciprocal_sqrt,
                        bias=eps[:],
                        scale=1.0 / STREAM_WIDTH,
                    )
                rstd_chunks.append(rstd)

            if 1 <= step <= CHUNKS:
                x_chunk = x_chunks[step - 1]
                rstd = rstd_chunks[step - 1]
                blocks = CHUNK_BLOCKS[step - 1]
                scaled = per_chunk.tile([P, blocks, D], F32, name="scaled")
                flipped_ps = banks.tile([D, blocks * P], F32, name="flipped_ps", tag="bank")
                for k in range(blocks):
                    nc.vector.tensor_scalar(scaled[:, k, :], x_chunk[:, k, :], rstd[:, k : k + 1], None, ALU.mult)
                    nc.tensor.transpose(flipped_ps[:, k * P : (k + 1) * P], scaled[:, k, :], identity[:])
                flipped_chunks.append(flipped_ps)

            if step >= 2:
                c = step - 2
                blocks = CHUNK_BLOCKS[c]
                table_part = table[:, FIRST_TOKEN[c] : FIRST_TOKEN[c] + blocks * P].rearrange("d (p k) -> d p k", k=blocks)
                in_token_order = flipped_chunks[c][:].rearrange("d (k p) -> d p k", k=blocks)
                if c in SCALAR_COPIES:
                    nc.scalar.activation(table_part, in_token_order, FUNC.Copy, scale=gain_col[:])
                else:
                    nc.vector.tensor_scalar(table_part, in_token_order, gain_col[:], None, ALU.mult)

        warm_gelu = held.tile([P, 1], F32, name="warm_gelu")
        nc.scalar.activation(warm_gelu[:], flipped_chunks[SCALAR_COPIES[-1]][:, 0:1], FUNC.Gelu)

        v_pieces = []
        for r in range(M_BLOCKS):
            wup_block = wup_sb[:, r * P : (r + 1) * P]
            if r == 0:
                pieces = []
                for i in range(2):
                    v_ps = banks.tile([P, N_HALF], F32, name="v_ps", tag="bank")
                    half_of_list = offsets[:, i * N_HALF // 16 : (i + 1) * N_HALF // 16]
                    nc.tensor.matmul(v_ps[:], wup_block, table[:].indirect(half_of_list), start=True, stop=True)
                    pieces.append((i * N_HALF, N_HALF, v_ps[:]))
            else:
                v_ps = banks.tile([P, N], F32, name="v_ps", tag="bank")
                nc.tensor.matmul(v_ps[:], wup_block, table[:].indirect(offsets[:]), start=True, stop=True)
                if r == M_BLOCKS - 1:
                    pieces = [(i * N_HALF, N_HALF, v_ps[:, i * N_HALF : (i + 1) * N_HALF]) for i in range(2)]
                else:
                    pieces = [(0, N, v_ps[:])]
            v_pieces.append(pieces)

        out_halves = [single.tile([D, N_HALF], F32, name=f"out_ps{i}") for i in range(2)]
        u = held.tile([P, M_BLOCKS, N], BF16, name="u")
        for r in range(M_BLOCKS):
            for first, tokens, v_piece in v_pieces[r]:
                nc.scalar.activation(u[:, r, first : first + tokens], v_piece, FUNC.Gelu, bias=bup_cols[:, r : r + 1])
            for i in range(2):
                nc.tensor.matmul(
                    out_halves[i][:],
                    wdown_sb[:, r, :],
                    u[:, r, i * N_HALF : (i + 1) * N_HALF],
                    start=(r == 0),
                    stop=(r == M_BLOCKS - 1),
                )

        result = held.tile([D, N], F32, name="result")
        for i in range(2):
            half = slice(i * N_HALF, (i + 1) * N_HALF)
            nc.vector.tensor_scalar(result[:, half], out_halves[i][:], bdown_col[:], None, ALU.add)
        for first, tokens in STORES:
            nc.sync.dma_start(out[:, first : first + tokens], result[:, first : first + tokens])
